import numpy as np
import ml_dtypes


def mxq(x, axis, fmt="e4m3"):
    dtype, down = {"e4m3": (ml_dtypes.float8_e4m3fn, 7), "e5m2": (ml_dtypes.float8_e5m2, 14)}[fmt]
    v = np.moveaxis(np.asarray(x, np.float32).astype(ml_dtypes.bfloat16).astype(np.float64), axis, -1)
    blocks = v.reshape(v.shape[:-1] + (-1, 32))
    amax = np.abs(blocks).max(-1, keepdims=True)
    byte = np.maximum(np.where(amax > 0, np.frexp(amax)[1] - 1 + 127, 0) - down, 1)
    scale = np.exp2(byte - 127.0)
    codes = (blocks / scale).astype(np.float32).astype(dtype).astype(np.float64)
    return np.moveaxis((codes * scale).reshape(v.shape), -1, axis)


WIDE = False


def mx_kscale(k):
    if not WIDE:
        return np.ones(k)
    levels = np.array([10, -10, 5, -5, 0])
    if k % 512:
        return np.exp2(np.random.permutation(np.resize(levels, k // 32))).repeat(32)
    a = np.empty((k // 512, 16))
    for p in range(k // 512):
        a[p, :8] = np.random.permutation(np.resize(levels, 8))
        for g in range(8):
            far = levels[np.abs(levels - a[p, g]) >= 10]
            a[p, g + 8] = far[np.random.randint(len(far))]
    return np.exp2(a.ravel()).repeat(32)


BF16 = ml_dtypes.bfloat16


def bf(x):
    return np.asarray(x, np.float32).astype(BF16)


def f64(x):
    return np.asarray(x).astype(np.float64)


N, M, D, R = 2048, 2048, 512, 4
LIM = 36.0


def softplus(v):
    return np.where(v > LIM, v, np.log(1.0 + np.exp(np.minimum(v, LIM))))


def setup_inputs():
    s = mx_kscale(N)
    u = mx_kscale(M)
    P = np.random.standard_normal((R, D))
    X0 = bf((0.6 * np.random.standard_normal((N, R)) @ P + 0.3 * np.random.standard_normal((N, D))) / np.sqrt(D))
    Z0 = bf((0.6 * np.random.standard_normal((M, R)) @ P + 0.3 * np.random.standard_normal((M, D))) / np.sqrt(D))
    l_raw = bf(np.random.uniform(0.0, 1.0, D))
    sigma_f_raw = bf(1.0 + 0.1 * np.random.standard_normal(1))
    g = bf(8.0 * np.random.standard_normal((N, M)) * np.exp2(np.random.randint(-6, 1, (N, 1))) / s[:, None] * u[None, :])
    l = softplus(f64(l_raw))
    w = np.sqrt(1.0 / (l * l))
    Xs = f64(X0) * w
    Zs = f64(Z0) * w
    x2 = np.sum(Xs * Xs, axis=1)
    z2 = np.sum(Zs * Zs, axis=1)
    arg = -0.5 * (x2[:, None] + z2[None, :] - 2.0 * (Xs @ Zs.T))
    return {"X": bf(f64(X0) * s[:, None]), "Z": bf(f64(Z0) / u[:, None]), "l_raw": l_raw, "sigma_f_raw": sigma_f_raw,
            "arg": np.asarray(arg, np.float32), "grad_out": g}


def reference(X, Z, l_raw, sigma_f_raw, arg, grad_out):
    l = softplus(f64(l_raw))
    sigma_f = softplus(f64(sigma_f_raw))
    w2 = 1.0 / (l * l)
    A = f64(grad_out) * (sigma_f * np.exp(f64(arg)))
    r = np.sum(A, axis=1)
    c = np.sum(A, axis=0)
    Ab = A
    AZ = mxq(Ab, 1, "e5m2") @ mxq(f64(Z), 0, "e4m3")
    AX = mxq(Ab, 0, "e5m2").T @ mxq(f64(X), 0, "e4m3")
    dX = (AZ - r[:, None] * f64(X)) * w2
    dZ = (AX - c[:, None] * f64(Z)) * w2
    return dX, dZ

@@ -1,0 +1,223 @@
+from contextlib import ExitStack
+
+import concourse.mybir as mybir
+from concourse.masks import make_identity
+
+N_TOK = 2048
+N_FEAT = 2048
+D = 512
+FLOPS = 2 * 2 * N_TOK * N_FEAT * D
+
+F32 = mybir.dt.float32
+BF16 = mybir.dt.bfloat16
+U32 = mybir.dt.uint32
+U8 = mybir.dt.uint8
+E4 = mybir.dt.float8_e4m3fn_x4
+E5 = mybir.dt.float8_e5m2_x4
+ALU = mybir.AluOpType
+ACT = mybir.ActivationFunctionType
+AX = mybir.AxisListType
+
+P = 128
+PACK = 4
+GRP = 512
+NG = 4
+LIM = 36.0
+ONES_N = 64
+
+
+def tile_rbf_kernel_v_kernel(tc, X, Z, l_raw, sigma_f_raw, arg, grad_out, out_0, out_1):
+    nc = tc.nc
+
+    x_v = X.rearrange("(g p t) d -> p g t d", p=P, t=PACK)
+    z_v = Z.rearrange("(g p t) d -> p g t d", p=P, t=PACK)
+    arg_v = arg.rearrange("(g p t) j -> p g t j", p=P, t=PACK)
+    go_v = grad_out.rearrange("(g p t) j -> p g t j", p=P, t=PACK)
+    o0_v = out_0.rearrange("(g p t) d -> p g t d", p=P, t=PACK)
+    o1_v = out_1.rearrange("(g p t) d -> p g t d", p=P, t=PACK)
+
+    with ExitStack() as ctx:
+        const = ctx.enter_context(tc.tile_pool(name="const", bufs=1))
+        keep = ctx.enter_context(tc.tile_pool(name="keep", bufs=1))
+        stream = ctx.enter_context(tc.tile_pool(name="stream", bufs=2))
+        ps_t = ctx.enter_context(tc.psum_pool(name="ps_t", bufs=4))
+        ps_c = ctx.enter_context(tc.psum_pool(name="ps_c", bufs=1))
+        ps_m = ctx.enter_context(tc.psum_pool(name="ps_m", bufs=3))
+
+        warm = const.tile([P, 1], F32, name="warm")
+        nc.vector.memset(warm[:], 0.0)
+        nc.scalar.activation(out=warm[:], in_=warm[:], func=ACT.Ln, bias=1.0)
+
+        lrow = const.tile([P, GRP + 32], BF16, name="lrow")
+        nc.vector.memset(lrow[:], 0.0)
+        nc.sync.dma_start(out=lrow[0:1, 0:GRP], in_=l_raw.rearrange("(o d) -> o d", o=1))
+        nc.sync.dma_start(out=lrow[0:1, GRP:GRP + 1], in_=sigma_f_raw.rearrange("(o d) -> o d", o=1))
+        ones_bf = const.tile([P, P], BF16, name="ones_bf")
+        nc.vector.memset(ones_bf[:], 1.0)
+        ones32 = const.tile([P, ONES_N], F32, name="ones32")
+        nc.vector.memset(ones32[:], 1.0)
+        ident = const.tile([P, P], F32, name="ident")
+        make_identity(nc, ident[:])
+
+        x_raw = keep.tile([P, NG, PACK, D], BF16, name="x_raw")
+        z_raw = keep.tile([P, NG, PACK, D], BF16, name="z_raw")
+        x_codes = keep.tile([P, NG, D], U32, name="x_codes", align_bytes=64)
+        x_scales = keep.tile([P, NG, D], U8, name="x_scales", align_bytes=64)
+        z_codes = keep.tile([P, NG, D], U32, name="z_codes", align_bytes=64)
+        z_scales = keep.tile([P, NG, D], U8, name="z_scales", align_bytes=64)
+        tok_codes = keep.tile([P, NG, N_FEAT], U32, name="tok_codes", align_bytes=64)
+        tok_scales = keep.tile([P, NG, N_FEAT], U8, name="tok_scales", align_bytes=64)
+        feat_codes = keep.tile([P, NG, N_TOK], U32, name="feat_codes", align_bytes=64)
+        feat_scales = keep.tile([P, NG, N_TOK], U8, name="feat_scales", align_bytes=64)
+        r_part = keep.tile([P, NG, PACK, NG], F32, name="r_part")
+        c_part = keep.tile([P, NG, PACK, NG], F32, name="c_part")
+
+        for k in range(NG):
+            nc.sync.dma_start(out=z_raw[:, k], in_=z_v[:, k])
+
+        ps_l = ps_m.tile([P, D], F32, name="acc", tag="acc")
+        nc.tensor.matmul(out=ps_l[:], lhsT=ones_bf[:], rhs=lrow[:, 0:GRP], start=True, stop=True)
+        ps_s = ps_m.tile([P, D], F32, name="acc", tag="acc")
+        nc.tensor.matmul(out=ps_s[:, 0:32], lhsT=ones_bf[:], rhs=lrow[:, GRP:GRP + 32], start=True, stop=True)
+        v_sb = const.tile([P, GRP + 32], F32, name="v_sb")
+        nc.vector.tensor_copy(out=v_sb[:, 0:GRP], in_=ps_l[:])
+        nc.vector.tensor_copy(out=v_sb[:, GRP:GRP + 32], in_=ps_s[:, 0:32])
+        sp = const.tile([P, GRP + 32], F32, name="sp")
+        nc.vector.tensor_scalar_min(out=sp[:], in0=v_sb[:], scalar1=LIM)
+        nc.scalar.activation(out=sp[:], in_=sp[:], func=ACT.Exp)
+        nc.scalar.activation(out=sp[:], in_=sp[:], func=ACT.Ln, bias=1.0)
+        nc.vector.tensor_tensor(out=sp[:], in0=sp[:], in1=v_sb[:], op=ALU.max)
+        sigma = const.tile([P, 1], F32, name="sigma")
+        nc.vector.tensor_copy(out=sigma[:], in_=sp[:, GRP:GRP + 1])
+        l_sq = const.tile([P, D], F32, name="l_sq")
+        nc.vector.tensor_tensor(out=l_sq[:], in0=sp[:, 0:GRP], in1=sp[:, 0:GRP], op=ALU.mult)
+        w2n = const.tile([P, D], F32, name="w2n")
+        nc.vector.reciprocal(out=w2n[:], in_=l_sq[:])
+        nc.vector.tensor_scalar_mul(out=w2n[:], in0=w2n[:], scalar1=-1.0)
+
+        def group_points(raw, k):
+            grouped = stream.tile([P, D, PACK], BF16, name="grouped", tag="grouped", bufs=3, align_bytes=64)
+            nc.vector.tensor_copy(
+                out=grouped[:].rearrange("p (c i) t -> p c t i", i=4),
+                in_=raw[:, k].rearrange("p t (c i) -> p c t i", i=4),
+            )
+            return grouped
+
+        def quantize_points(grouped, codes, scales, k):
+            nc.vector.quantize_mx(
+                out=codes[:, k, :].bitcast(E4),
+                scales=scales[:, k, :],
+                in_=grouped[:].rearrange("p d t -> p (d t)"),
+            )
+
+        def chunk(g, G):
+            cols = slice(G * GRP, (G + 1) * GRP)
+            rows = slice(g * GRP, (g + 1) * GRP)
+            e_t = stream.tile([P, PACK, GRP], F32, name="e_t", tag="e_t", bufs=3)
+            nc.sync.dma_start(out=e_t[:], in_=arg_v[:, g, :, cols])
+            g_t = stream.tile([P, PACK, GRP], BF16, name="g_t", tag="g_t", bufs=3)
+            nc.sync.dma_start(out=g_t[:], in_=go_v[:, g, :, cols])
+
+            nc.scalar.activation(out=e_t[:], in_=e_t[:], func=ACT.Exp)
+
+            a32 = stream.tile([P, PACK, GRP], F32, name="a32", tag="a32", bufs=2)
+            for t in range(PACK):
+                nc.vector.scalar_tensor_tensor(
+                    out=a32[:, t, :].rearrange("p (u m) -> p u m", u=PACK),
+                    in0=e_t[:, t, :].rearrange("p (m u) -> p u m", u=PACK),
+                    scalar=sigma[:],
+                    in1=g_t[:, t, :].rearrange("p (m u) -> p u m", u=PACK),
+                    op0=ALU.mult,
+                    op1=ALU.mult,
+                    accum_out=r_part[:, g, t, G:G + 1],
+                )
+
+            grouped = stream.tile([P, GRP, PACK], BF16, name="grouped", tag="grouped", bufs=3, align_bytes=64)
+            nc.scalar.copy(
+                out=grouped[:].rearrange("p (c i) t -> p c t i", i=4),
+                in_=a32[:].rearrange("p t (c i) -> p c t i", i=4),
+            )
+            nc.vector.quantize_mx(
+                out=tok_codes[:, g, cols].bitcast(E5),
+                scales=tok_scales[:, g, cols],
+                in_=grouped[:].rearrange("p c t -> p (c t)"),
+            )
+
+            fin = stream.tile([P, PACK, P, PACK], BF16, name="fin", tag="fin", bufs=2, align_bytes=64)
+            for t in range(PACK):
+                bank = ps_t.tile([P, PACK, P], F32, name="bank", tag="bank")
+                for u in range(PACK):
+                    nc.tensor.transpose(out=bank[:, u, :], in_=a32[:, t, u * P:(u + 1) * P], identity=ident[:])
+                nc.scalar.copy(out=fin[:, t], in_=bank[:].rearrange("m u p -> m p u"))
+
+            c_bank = ps_c.tile([P, PACK, ONES_N], F32, name="c_bank", tag="c_bank")
+            for u in range(PACK):
+                for t in range(PACK):
+                    nc.tensor.matmul(
+                        out=c_bank[:, u, :],
+                        lhsT=a32[:, t, u * P:(u + 1) * P],
+                        rhs=ones32[:],
+                        start=(t == 0),
+                        stop=(t == PACK - 1),
+                    )
+            nc.vector.tensor_copy(out=c_part[:, G, :, g], in_=c_bank[:, :, 0])
+
+            nc.vector.quantize_mx(
+                out=feat_codes[:, G, rows].bitcast(E5),
+                scales=feat_scales[:, G, rows],
+                in_=fin[:].rearrange("m t p u -> m (t p u)"),
+            )
+
+        def finish(a_codes, a_scales, b_codes, b_scales, raw, part, out_v, s, store):
+            sums = stream.tile([P, PACK], F32, name="sums", tag="sums", bufs=2)
+            nc.vector.tensor_reduce(out=sums[:], in_=part[:, s], axis=AX.X, op=ALU.add)
+            for t in range(PACK):
+                m_cols = slice(s * GRP + t * P, s * GRP + (t + 1) * P)
+                acc = ps_m.tile([P, D], F32, name="acc", tag="acc")
+                for k in range(NG):
+                    nc.tensor.matmul_mx(
+                        out=acc[:],
+                        lhsT=a_codes[:, k, m_cols].bitcast(E5),
+                        lhsT_scale=a_scales[:, k, m_cols],
+                        rhs=b_codes[:, k, :].bitcast(E4),
+                        rhs_scale=b_scales[:, k, :],
+                        start=(k == 0),
+                        stop=(k == NG - 1),
+                    )
+                diff = stream.tile([P, D], F32, name="diff", tag="diff", bufs=2)
+                nc.vector.scalar_tensor_tensor(
+                    out=diff[:], in0=raw[:, s, t, :], scalar=sums[:, t:t + 1], in1=acc[:],
+                    op0=ALU.mult, op1=ALU.subtract,
+                )
+                res = stream.tile([P, D], F32, name="res", tag="res", bufs=4)
+                nc.vector.tensor_tensor(out=res[:], in0=diff[:], in1=w2n[:], op=ALU.mult)
+                store(out=out_v[:, s, t, :], in_=res[:])
+
+        z_grouped = [group_points(z_raw, 0)]
+        for k in range(NG):
+            if k + 1 < NG:
+                z_grouped.append(group_points(z_raw, k + 1))
+            quantize_points(z_grouped[k], z_codes, z_scales, k)
+
+        order = []
+        for s in range(NG):
+            for G in range(s, NG):
+                order.append((s, G))
+            for g in range(s + 1, NG):
+                order.append((g, s))
+
+        row_count = [0] * NG
+        col_count = [0] * NG
+        for i, (g, G) in enumerate(order):
+            chunk(g, G)
+            if i < NG:
+                nc.sync.dma_start(out=x_raw[:, i], in_=x_v[:, i])
+                quantize_points(group_points(x_raw, i), x_codes, x_scales, i)
+            row_count[g] = row_count[g] + 1
+            col_count[G] = col_count[G] + 1
+            if row_count[g] == NG:
+                finish(feat_codes, feat_scales, z_codes, z_scales, x_raw, r_part, o0_v, g,
+                       nc.sync.dma_start if g == NG - 1 else nc.gpsimd.dma_start)
+            if col_count[G] == NG:
+                finish(tok_codes, tok_scales, x_codes, x_scales, z_raw, c_part, o1_v, G,
+                       nc.sync.dma_start if G == NG - 1 else nc.gpsimd.dma_start)

@@ -22,8 +22,10 @@ P = 128
 PACK = 4
 GRP = 512
 NG = 4
+NC = NG * NG
 LIM = 36.0
-ONES_N = 64
+MX_PER_STEP = 3
+CASTS_ON_VECTOR = 12
 
 
 def tile_rbf_kernel_v_kernel(tc, X, Z, l_raw, sigma_f_raw, arg, grad_out, out_0, out_1):
@@ -31,10 +33,29 @@ def tile_rbf_kernel_v_kernel(tc, X, Z, l_raw, sigma_f_raw, arg, grad_out, out_0,
 
     x_v = X.rearrange("(g p t) d -> p g t d", p=P, t=PACK)
     z_v = Z.rearrange("(g p t) d -> p g t d", p=P, t=PACK)
+    z_nat_v = Z.rearrange("(g b p) d -> p g b d", p=P, b=PACK)
     arg_v = arg.rearrange("(g p t) j -> p g t j", p=P, t=PACK)
     go_v = grad_out.rearrange("(g p t) j -> p g t j", p=P, t=PACK)
     o0_v = out_0.rearrange("(g p t) d -> p g t d", p=P, t=PACK)
-    o1_v = out_1.rearrange("(g p t) d -> p g t d", p=P, t=PACK)
+    o1_v = out_1.rearrange("(g b p) d -> p g b d", p=P, b=PACK)
+
+    order = []
+    for s in range(NG):
+        for G in range(s, NG):
+            order.append((s, G))
+        for g in range(s + 1, NG):
+            order.append((g, s))
+    row_done = {}
+    col_done = {}
+    row_count = [0] * NG
+    col_count = [0] * NG
+    for c, (g, G) in enumerate(order):
+        row_count[g] = row_count[g] + 1
+        col_count[G] = col_count[G] + 1
+        if row_count[g] == NG:
+            row_done[c] = g
+        if col_count[G] == NG:
+            col_done[c] = G
 
     with ExitStack() as ctx:
         const = ctx.enter_context(tc.tile_pool(name="const", bufs=1))
@@ -43,24 +64,10 @@ def tile_rbf_kernel_v_kernel(tc, X, Z, l_raw, sigma_f_raw, arg, grad_out, out_0,
         ps_t = ctx.enter_context(tc.psum_pool(name="ps_t", bufs=4))
         ps_c = ctx.enter_context(tc.psum_pool(name="ps_c", bufs=1))
         ps_m = ctx.enter_context(tc.psum_pool(name="ps_m", bufs=3))
-
-        warm = const.tile([P, 1], F32, name="warm")
-        nc.vector.memset(warm[:], 0.0)
-        nc.scalar.activation(out=warm[:], in_=warm[:], func=ACT.Ln, bias=1.0)
-
-        lrow = const.tile([P, GRP + 32], BF16, name="lrow")
-        nc.vector.memset(lrow[:], 0.0)
-        nc.sync.dma_start(out=lrow[0:1, 0:GRP], in_=l_raw.rearrange("(o d) -> o d", o=1))
-        nc.sync.dma_start(out=lrow[0:1, GRP:GRP + 1], in_=sigma_f_raw.rearrange("(o d) -> o d", o=1))
-        ones_bf = const.tile([P, P], BF16, name="ones_bf")
-        nc.vector.memset(ones_bf[:], 1.0)
-        ones32 = const.tile([P, ONES_N], F32, name="ones32")
-        nc.vector.memset(ones32[:], 1.0)
-        ident = const.tile([P, P], F32, name="ident")
-        make_identity(nc, ident[:])
+        ctx.enter_context(tc.manual_schedule())
 
         x_raw = keep.tile([P, NG, PACK, D], BF16, name="x_raw")
-        z_raw = keep.tile([P, NG, PACK, D], BF16, name="z_raw")
+        z_nat = keep.tile([P, NG, PACK, D], BF16, name="z_nat")
         x_codes = keep.tile([P, NG, D], U32, name="x_codes", align_bytes=64)
         x_scales = keep.tile([P, NG, D], U8, name="x_scales", align_bytes=64)
         z_codes = keep.tile([P, NG, D], U32, name="z_codes", align_bytes=64)
@@ -72,8 +79,59 @@ def tile_rbf_kernel_v_kernel(tc, X, Z, l_raw, sigma_f_raw, arg, grad_out, out_0,
         r_part = keep.tile([P, NG, PACK, NG], F32, name="r_part")
         c_part = keep.tile([P, NG, PACK, NG], F32, name="c_part")
 
-        for k in range(NG):
-            nc.sync.dma_start(out=z_raw[:, k], in_=z_v[:, k])
+        e_tiles = {}
+        g_tiles = {}
+        a_tiles = {}
+        abf_tiles = {}
+        grouped_tiles = {}
+        fin_tiles = {}
+        bank_tiles = {}
+        c_banks = {}
+
+        def load(c):
+            g, G = order[c]
+            cols = slice(G * GRP, (G + 1) * GRP)
+            e_t = stream.tile([P, PACK, GRP], F32, name="e_t", tag="e_t", bufs=3)
+            nc.sync.dma_start(out=e_t[:], in_=arg_v[:, g, :, cols])
+            g_t = stream.tile([P, PACK, GRP], BF16, name="g_t", tag="g_t", bufs=3)
+            nc.sync.dma_start(out=g_t[:], in_=go_v[:, g, :, cols])
+            e_tiles[c] = e_t
+            g_tiles[c] = g_t
+
+        warm = const.tile([P, 1], F32, name="warm")
+        nc.vector.memset(warm[:], 0.0)
+        nc.scalar.activation(out=warm[:], in_=warm[:], func=ACT.Exp)
+        lrow = const.tile([P, GRP + 32], BF16, name="lrow")
+        nc.vector.memset(lrow[:], 0.0)
+        nc.sync.dma_start(out=lrow[0:1, 0:GRP], in_=l_raw.rearrange("(o d) -> o d", o=1))
+        nc.sync.dma_start(out=lrow[0:1, GRP:GRP + 1], in_=sigma_f_raw.rearrange("(o d) -> o d", o=1))
+        ones_bf = const.tile([P, P], BF16, name="ones_bf")
+        nc.vector.memset(ones_bf[:], 1.0)
+        ident = const.tile([P, P], F32, name="ident")
+        make_identity(nc, ident[:])
+
+        z_tiles = {}
+
+        def load_z(k):
+            z_t = stream.tile([P, PACK, D], BF16, name="fin", tag="fin", bufs=2, align_bytes=64)
+            nc.sync.dma_start(out=z_t[:], in_=z_v[:, k])
+            z_tiles[k] = z_t
+
+        def group_points(raw_k, key):
+            grouped = stream.tile([P, D, PACK], BF16, name="grouped", tag="grouped", bufs=3, align_bytes=64)
+            nc.vector.tensor_copy(out=grouped[:], in_=raw_k.rearrange("p t d -> p d t"))
+            grouped_tiles[key] = grouped
+
+        def quantize_points(key, codes, scales, k):
+            nc.vector.quantize_mx(
+                out=codes[:, k, :].bitcast(E4),
+                scales=scales[:, k, :],
+                in_=grouped_tiles[key][:].rearrange("p d t -> p (d t)"),
+            )
+
+        load_z(0)
+        load_z(1)
+        load(0)
 
         ps_l = ps_m.tile([P, D], F32, name="acc", tag="acc")
         nc.tensor.matmul(out=ps_l[:], lhsT=ones_bf[:], rhs=lrow[:, 0:GRP], start=True, stop=True)
@@ -86,138 +144,195 @@ def tile_rbf_kernel_v_kernel(tc, X, Z, l_raw, sigma_f_raw, arg, grad_out, out_0,
         nc.vector.tensor_scalar_min(out=sp[:], in0=v_sb[:], scalar1=LIM)
         nc.scalar.activation(out=sp[:], in_=sp[:], func=ACT.Exp)
         nc.scalar.activation(out=sp[:], in_=sp[:], func=ACT.Ln, bias=1.0)
+
+        group_points(z_tiles[0][:], "z0")
+        group_points(z_tiles[1][:], "z1")
+        load_z(2)
+        load_z(3)
+        load(1)
+        load(2)
+        quantize_points("z0", z_codes, z_scales, 0)
+        quantize_points("z1", z_codes, z_scales, 1)
+
         nc.vector.tensor_tensor(out=sp[:], in0=sp[:], in1=v_sb[:], op=ALU.max)
         sigma = const.tile([P, 1], F32, name="sigma")
         nc.vector.tensor_copy(out=sigma[:], in_=sp[:, GRP:GRP + 1])
-        l_sq = const.tile([P, D], F32, name="l_sq")
-        nc.vector.tensor_tensor(out=l_sq[:], in0=sp[:, 0:GRP], in1=sp[:, 0:GRP], op=ALU.mult)
+        nc.vector.tensor_tensor(out=v_sb[:, 0:GRP], in0=sp[:, 0:GRP], in1=sp[:, 0:GRP], op=ALU.mult)
         w2n = const.tile([P, D], F32, name="w2n")
-        nc.vector.reciprocal(out=w2n[:], in_=l_sq[:])
+        nc.vector.reciprocal(out=w2n[:], in_=v_sb[:, 0:GRP])
         nc.vector.tensor_scalar_mul(out=w2n[:], in0=w2n[:], scalar1=-1.0)
 
-        def group_points(raw, k):
-            grouped = stream.tile([P, D, PACK], BF16, name="grouped", tag="grouped", bufs=3, align_bytes=64)
-            nc.vector.tensor_copy(
-                out=grouped[:].rearrange("p (c i) t -> p c t i", i=4),
-                in_=raw[:, k].rearrange("p t (c i) -> p c t i", i=4),
-            )
-            return grouped
+        group_points(z_tiles[2][:], "z2")
+        group_points(z_tiles[3][:], "z3")
+        quantize_points("z2", z_codes, z_scales, 2)
+        quantize_points("z3", z_codes, z_scales, 3)
+        for k in range(NG):
+            nc.sync.dma_start(out=x_raw[:, k], in_=x_v[:, k])
 
-        def quantize_points(grouped, codes, scales, k):
-            nc.vector.quantize_mx(
-                out=codes[:, k, :].bitcast(E4),
-                scales=scales[:, k, :],
-                in_=grouped[:].rearrange("p d t -> p (d t)"),
-            )
+        def exp(c):
+            nc.scalar.activation(out=e_tiles[c][:], in_=e_tiles[c][:], func=ACT.Exp)
 
-        def chunk(g, G):
-            cols = slice(G * GRP, (G + 1) * GRP)
-            rows = slice(g * GRP, (g + 1) * GRP)
-            e_t = stream.tile([P, PACK, GRP], F32, name="e_t", tag="e_t", bufs=3)
-            nc.sync.dma_start(out=e_t[:], in_=arg_v[:, g, :, cols])
-            g_t = stream.tile([P, PACK, GRP], BF16, name="g_t", tag="g_t", bufs=3)
-            nc.sync.dma_start(out=g_t[:], in_=go_v[:, g, :, cols])
-
-            nc.scalar.activation(out=e_t[:], in_=e_t[:], func=ACT.Exp)
-
+        def mult(c):
+            g, G = order[c]
             a32 = stream.tile([P, PACK, GRP], F32, name="a32", tag="a32", bufs=2)
+            a_tiles[c] = a32
             for t in range(PACK):
                 nc.vector.scalar_tensor_tensor(
-                    out=a32[:, t, :].rearrange("p (u m) -> p u m", u=PACK),
-                    in0=e_t[:, t, :].rearrange("p (m u) -> p u m", u=PACK),
-                    scalar=sigma[:],
-                    in1=g_t[:, t, :].rearrange("p (m u) -> p u m", u=PACK),
-                    op0=ALU.mult,
-                    op1=ALU.mult,
-                    accum_out=r_part[:, g, t, G:G + 1],
+                    out=a32[:, t, :], in0=e_tiles[c][:, t, :], scalar=sigma[:], in1=g_tiles[c][:, t, :],
+                    op0=ALU.mult, op1=ALU.mult, accum_out=r_part[:, g, t, G:G + 1],
                 )
 
+        def cast(c):
+            abf = stream.tile([P, PACK, GRP], BF16, name="abf", tag="abf", bufs=2)
+            abf_tiles[c] = abf
+            if c < CASTS_ON_VECTOR:
+                nc.vector.tensor_copy(out=abf[:], in_=a_tiles[c][:])
+            else:
+                nc.scalar.copy(out=abf[:], in_=a_tiles[c][:])
+
+        def group_tokens(c):
             grouped = stream.tile([P, GRP, PACK], BF16, name="grouped", tag="grouped", bufs=3, align_bytes=64)
-            nc.scalar.copy(
-                out=grouped[:].rearrange("p (c i) t -> p c t i", i=4),
-                in_=a32[:].rearrange("p t (c i) -> p c t i", i=4),
-            )
+            grouped_tiles[c] = grouped
+            nc.scalar.copy(out=grouped[:], in_=abf_tiles[c][:].rearrange("p t c -> p c t"))
+
+        def quantize_tokens(c):
+            g, G = order[c]
+            cols = slice(G * GRP, (G + 1) * GRP)
             nc.vector.quantize_mx(
                 out=tok_codes[:, g, cols].bitcast(E5),
                 scales=tok_scales[:, g, cols],
-                in_=grouped[:].rearrange("p c t -> p (c t)"),
+                in_=grouped_tiles[c][:].rearrange("p c t -> p (c t)"),
             )
 
-            fin = stream.tile([P, PACK, P, PACK], BF16, name="fin", tag="fin", bufs=2, align_bytes=64)
-            for t in range(PACK):
-                bank = ps_t.tile([P, PACK, P], F32, name="bank", tag="bank")
-                for u in range(PACK):
-                    nc.tensor.transpose(out=bank[:, u, :], in_=a32[:, t, u * P:(u + 1) * P], identity=ident[:])
-                nc.scalar.copy(out=fin[:, t], in_=bank[:].rearrange("m u p -> m p u"))
+        def transposes(c):
+            for h in range(2):
+                bank = ps_t.tile([P, 2, 2, P], F32, name="bank", tag="bank")
+                bank_tiles[(c, h)] = bank
+                for t2 in range(2):
+                    words = abf_tiles[c][:, 2 * h + t2, :].bitcast(F32)
+                    for v in range(2):
+                        nc.tensor.transpose(out=bank[:, t2, v, :], in_=words[:, v:GRP // 2:2], identity=ident[:])
 
-            c_bank = ps_c.tile([P, PACK, ONES_N], F32, name="c_bank", tag="c_bank")
-            for u in range(PACK):
+        def column_sums(c):
+            c_bank = ps_c.tile([P, PACK, P], F32, name="c_bank", tag="c_bank")
+            c_banks[c] = c_bank
+            for b in range(PACK):
                 for t in range(PACK):
                     nc.tensor.matmul(
-                        out=c_bank[:, u, :],
-                        lhsT=a32[:, t, u * P:(u + 1) * P],
-                        rhs=ones32[:],
-                        start=(t == 0),
-                        stop=(t == PACK - 1),
+                        out=c_bank[:, b, :], lhsT=a_tiles[c][:, t, b * P:(b + 1) * P], rhs=ident[:],
+                        is_transpose=True, start=(t == 0), stop=(t == PACK - 1),
                     )
-            nc.vector.tensor_copy(out=c_part[:, G, :, g], in_=c_bank[:, :, 0])
 
+        def keep_column_sums(c):
+            g, G = order[c]
+            nc.vector.tensor_reduce(out=c_part[:, G, :, g], in_=c_banks[c][:], axis=AX.X, op=ALU.add)
+
+        def group_features(c):
+            fin = stream.tile([P, PACK, P, PACK], BF16, name="fin", tag="fin", bufs=2, align_bytes=64)
+            fin_tiles[c] = fin
+            for h in range(2):
+                fin_words = fin[:, 2 * h:2 * h + 2].rearrange("m t p u -> m (t p u)").bitcast(F32)
+                nc.scalar.copy(
+                    out=fin_words.rearrange("m (t p v) -> m t p v", t=2, v=2),
+                    in_=bank_tiles[(c, h)][:].rearrange("m t v p -> m t p v"),
+                )
+
+        def quantize_features(c):
+            g, G = order[c]
+            rows = slice(g * GRP, (g + 1) * GRP)
             nc.vector.quantize_mx(
                 out=feat_codes[:, G, rows].bitcast(E5),
                 scales=feat_scales[:, G, rows],
-                in_=fin[:].rearrange("m t p u -> m (t p u)"),
+                in_=fin_tiles[c][:].rearrange("m t p u -> m (t p u)"),
             )
 
-        def finish(a_codes, a_scales, b_codes, b_scales, raw, part, out_v, s, store):
-            sums = stream.tile([P, PACK], F32, name="sums", tag="sums", bufs=2)
-            nc.vector.tensor_reduce(out=sums[:], in_=part[:, s], axis=AX.X, op=ALU.add)
-            for t in range(PACK):
-                m_cols = slice(s * GRP + t * P, s * GRP + (t + 1) * P)
-                acc = ps_m.tile([P, D], F32, name="acc", tag="acc")
-                for k in range(NG):
-                    nc.tensor.matmul_mx(
-                        out=acc[:],
-                        lhsT=a_codes[:, k, m_cols].bitcast(E5),
-                        lhsT_scale=a_scales[:, k, m_cols],
-                        rhs=b_codes[:, k, :].bitcast(E4),
-                        rhs_scale=b_scales[:, k, :],
-                        start=(k == 0),
-                        stop=(k == NG - 1),
-                    )
-                diff = stream.tile([P, D], F32, name="diff", tag="diff", bufs=2)
-                nc.vector.scalar_tensor_tensor(
-                    out=diff[:], in0=raw[:, s, t, :], scalar=sums[:, t:t + 1], in1=acc[:],
-                    op0=ALU.mult, op1=ALU.subtract,
+        sums_tiles = {}
+
+        def product(kind, s, t):
+            if kind == 0:
+                a_codes, a_scales, b_codes, b_scales, part = feat_codes, feat_scales, z_codes, z_scales, r_part
+            else:
+                a_codes, a_scales, b_codes, b_scales, part = tok_codes, tok_scales, x_codes, x_scales, c_part
+            if t == 0:
+                sums = stream.tile([P, PACK], F32, name="sums", tag="sums", bufs=3)
+                nc.vector.tensor_reduce(out=sums[:], in_=part[:, s], axis=AX.X, op=ALU.add)
+                sums_tiles[(kind, s)] = sums
+            m_cols = slice(s * GRP + t * P, s * GRP + (t + 1) * P)
+            acc = ps_m.tile([P, D], F32, name="acc", tag="acc")
+            for k in range(NG):
+                nc.tensor.matmul_mx(
+                    out=acc[:],
+                    lhsT=a_codes[:, k, m_cols].bitcast(E5), lhsT_scale=a_scales[:, k, m_cols],
+                    rhs=b_codes[:, k, :].bitcast(E4), rhs_scale=b_scales[:, k, :],
+                    start=(k == 0), stop=(k == NG - 1),
                 )
-                res = stream.tile([P, D], F32, name="res", tag="res", bufs=4)
-                nc.vector.tensor_tensor(out=res[:], in0=diff[:], in1=w2n[:], op=ALU.mult)
-                store(out=out_v[:, s, t, :], in_=res[:])
+            return (kind, s, t, acc)
 
-        z_grouped = [group_points(z_raw, 0)]
-        for k in range(NG):
-            if k + 1 < NG:
-                z_grouped.append(group_points(z_raw, k + 1))
-            quantize_points(z_grouped[k], z_codes, z_scales, k)
+        def subtract_sum_term(item):
+            kind, s, t, acc = item
+            raw = x_raw if kind == 0 else z_nat
+            diff = stream.tile([P, D], F32, name="diff", tag="diff", bufs=3)
+            nc.vector.scalar_tensor_tensor(
+                out=diff[:], in0=raw[:, s, t, :], scalar=sums_tiles[(kind, s)][:, t:t + 1], in1=acc[:],
+                op0=ALU.mult, op1=ALU.subtract,
+            )
+            return (kind, s, t, diff)
 
-        order = []
-        for s in range(NG):
-            for G in range(s, NG):
-                order.append((s, G))
-            for g in range(s + 1, NG):
-                order.append((g, s))
+        def scale_and_store(item):
+            kind, s, t, diff = item
+            out_v = o0_v if kind == 0 else o1_v
+            res = stream.tile([P, D], F32, name="res", tag="res", bufs=4)
+            nc.vector.tensor_tensor(out=res[:], in0=diff[:], in1=w2n[:], op=ALU.mult)
+            nc.sync.dma_start(out=out_v[:, s, t, :], in_=res[:])
 
-        row_count = [0] * NG
-        col_count = [0] * NG
-        for i, (g, G) in enumerate(order):
-            chunk(g, G)
-            if i < NG:
-                nc.sync.dma_start(out=x_raw[:, i], in_=x_v[:, i])
-                quantize_points(group_points(x_raw, i), x_codes, x_scales, i)
-            row_count[g] = row_count[g] + 1
-            col_count[G] = col_count[G] + 1
-            if row_count[g] == NG:
-                finish(feat_codes, feat_scales, z_codes, z_scales, x_raw, r_part, o0_v, g,
-                       nc.sync.dma_start if g == NG - 1 else nc.gpsimd.dma_start)
-            if col_count[G] == NG:
-                finish(tok_codes, tok_scales, x_codes, x_scales, z_raw, c_part, o1_v, G,
-                       nc.sync.dma_start if G == NG - 1 else nc.gpsimd.dma_start)
+        ready = []
+        in_flight = []
+        k = -2
+        while k < NC + 1 or ready or in_flight:
+            if 3 <= k + 3 < NC:
+                load(k + 3)
+            if 0 <= k < NG:
+                nc.sync.dma_start(out=z_nat[:, k], in_=z_nat_v[:, k])
+            if 0 <= k + 2 < NC:
+                exp(k + 2)
+            if 0 <= k < NC:
+                transposes(k)
+            if 0 <= k - 1 < NC:
+                quantize_features(k - 1)
+                if (k - 1) in row_done:
+                    for t in range(PACK):
+                        ready.append((0, row_done[k - 1], t))
+            if 0 <= k < NC:
+                keep_column_sums(k)
+            if 0 <= k < NG:
+                group_points(x_raw[:, k], "x%d" % k)
+            if 0 <= k + 1 < NC:
+                mult(k + 1)
+                column_sums(k + 1)
+            if 0 <= k < NC:
+                group_tokens(k)
+            if 0 <= k < NG:
+                quantize_points("x%d" % k, x_codes, x_scales, k)
+            waiting = []
+            for item in in_flight:
+                waiting.append(subtract_sum_term(item))
+                if len(waiting) > 1:
+                    scale_and_store(waiting.pop(0))
+            in_flight = []
+            if 0 <= k + 1 < CASTS_ON_VECTOR:
+                cast(k + 1)
+            if waiting:
+                scale_and_store(waiting.pop(0))
+            if 0 <= k < NC:
+                quantize_tokens(k)
+                if k in col_done:
+                    for t in range(PACK):
+                        ready.append((1, col_done[k], t))
+            while ready and len(in_flight) < (2 if k < 12 else MX_PER_STEP):
+                kind, s, t = ready.pop(0)
+                in_flight.append(product(kind, s, t))
+            if 0 <= k < NC:
+                group_features(k)
+            if CASTS_ON_VECTOR <= k + 1 < NC:
+                cast(k + 1)
+            k = k + 1

@@ -119,7 +119,10 @@ def tile_rbf_kernel_v_kernel(tc, X, Z, l_raw, sigma_f_raw, arg, grad_out, out_0,
 
         def group_points(raw_k, key):
             grouped = stream.tile([P, D, PACK], BF16, name="grouped", tag="grouped", bufs=3, align_bytes=64)
-            nc.vector.tensor_copy(out=grouped[:], in_=raw_k.rearrange("p t d -> p d t"))
+            nc.vector.tensor_copy(
+                out=grouped[:].rearrange("p (c i) t -> p c t i", i=4),
+                in_=raw_k.rearrange("p t (c i) -> p c t i", i=4),
+            )
             grouped_tiles[key] = grouped
 
         def quantize_points(key, codes, scales, k):
@@ -193,7 +196,10 @@ def tile_rbf_kernel_v_kernel(tc, X, Z, l_raw, sigma_f_raw, arg, grad_out, out_0,
         def group_tokens(c):
             grouped = stream.tile([P, GRP, PACK], BF16, name="grouped", tag="grouped", bufs=3, align_bytes=64)
             grouped_tiles[c] = grouped
-            nc.scalar.copy(out=grouped[:], in_=abf_tiles[c][:].rearrange("p t c -> p c t"))
+            nc.scalar.copy(
+                out=grouped[:].rearrange("p (c i) t -> p c t i", i=4),
+                in_=abf_tiles[c][:].rearrange("p t (c i) -> p c t i", i=4),
+            )
 
         def quantize_tokens(c):
             g, G = order[c]

@@ -25,7 +25,7 @@ NG = 4
 NC = NG * NG
 LIM = 36.0
 MX_PER_STEP = 3
-CASTS_ON_VECTOR = 12
+LAST_SHARED_CAST = 13
 
 
 def tile_rbf_kernel_v_kernel(tc, X, Z, l_raw, sigma_f_raw, arg, grad_out, out_0, out_1):
@@ -153,6 +153,7 @@ def tile_rbf_kernel_v_kernel(tc, X, Z, l_raw, sigma_f_raw, arg, grad_out, out_0,
         load_z(2)
         load_z(3)
         load(1)
+        nc.sync.dma_start(out=x_raw[:, 0], in_=x_v[:, 0])
         load(2)
         quantize_points("z0", z_codes, z_scales, 0)
         quantize_points("z1", z_codes, z_scales, 1)
@@ -169,7 +170,7 @@ def tile_rbf_kernel_v_kernel(tc, X, Z, l_raw, sigma_f_raw, arg, grad_out, out_0,
         group_points(z_tiles[3][:], "z3")
         quantize_points("z2", z_codes, z_scales, 2)
         quantize_points("z3", z_codes, z_scales, 3)
-        for k in range(NG):
+        for k in range(1, NG):
             nc.sync.dma_start(out=x_raw[:, k], in_=x_v[:, k])
 
         def exp(c):
@@ -185,13 +186,20 @@ def tile_rbf_kernel_v_kernel(tc, X, Z, l_raw, sigma_f_raw, arg, grad_out, out_0,
                     op0=ALU.mult, op1=ALU.mult, accum_out=r_part[:, g, t, G:G + 1],
                 )
 
-        def cast(c):
-            abf = stream.tile([P, PACK, GRP], BF16, name="abf", tag="abf", bufs=2)
-            abf_tiles[c] = abf
-            if c < CASTS_ON_VECTOR:
-                nc.vector.tensor_copy(out=abf[:], in_=a_tiles[c][:])
-            else:
-                nc.scalar.copy(out=abf[:], in_=a_tiles[c][:])
+        def cast_on_vector(c, h):
+            return c < LAST_SHARED_CAST and (c % 2 == 0 or h == 1)
+
+        def cast(c, on_vector):
+            if c not in abf_tiles:
+                abf = stream.tile([P, PACK, GRP], BF16, name="abf", tag="abf", bufs=2)
+                abf_tiles[c] = abf
+            for h in range(2):
+                if cast_on_vector(c, h) == on_vector:
+                    rows = slice(2 * h, 2 * h + 2)
+                    if on_vector:
+                        nc.vector.tensor_copy(out=abf_tiles[c][:, rows], in_=a_tiles[c][:, rows])
+                    else:
+                        nc.scalar.copy(out=abf_tiles[c][:, rows], in_=a_tiles[c][:, rows])
 
         def group_tokens(c):
             grouped = stream.tile([P, GRP, PACK], BF16, name="grouped", tag="grouped", bufs=3, align_bytes=64)
@@ -308,12 +316,13 @@ def tile_rbf_kernel_v_kernel(tc, X, Z, l_raw, sigma_f_raw, arg, grad_out, out_0,
                 if (k - 1) in row_done:
                     for t in range(PACK):
                         ready.append((0, row_done[k - 1], t))
-            if 0 <= k < NC:
-                keep_column_sums(k)
             if 0 <= k < NG:
                 group_points(x_raw[:, k], "x%d" % k)
             if 0 <= k + 1 < NC:
                 mult(k + 1)
+            if 0 <= k < NC:
+                keep_column_sums(k)
+            if 0 <= k + 1 < NC:
                 column_sums(k + 1)
             if 0 <= k < NC:
                 group_tokens(k)
@@ -325,8 +334,8 @@ def tile_rbf_kernel_v_kernel(tc, X, Z, l_raw, sigma_f_raw, arg, grad_out, out_0,
                 if len(waiting) > 1:
                     scale_and_store(waiting.pop(0))
             in_flight = []
-            if 0 <= k + 1 < CASTS_ON_VECTOR:
-                cast(k + 1)
+            if 0 <= k + 1 < NC:
+                cast(k + 1, True)
             if waiting:
                 scale_and_store(waiting.pop(0))
             if 0 <= k < NC:
@@ -339,6 +348,6 @@ def tile_rbf_kernel_v_kernel(tc, X, Z, l_raw, sigma_f_raw, arg, grad_out, out_0,
                 in_flight.append(product(kind, s, t))
             if 0 <= k < NC:
                 group_features(k)
-            if CASTS_ON_VECTOR <= k + 1 < NC:
-                cast(k + 1)
+            if 0 <= k + 1 < NC:
+                cast(k + 1, False)
             k = k + 1

@@ -303,8 +303,6 @@ def tile_rbf_kernel_v_kernel(tc, X, Z, l_raw, sigma_f_raw, arg, grad_out, out_0,
         in_flight = []
         k = -2
         while k < NC + 1 or ready or in_flight:
-            if 3 <= k + 3 < NC:
-                load(k + 3)
             if 0 <= k < NG:
                 nc.sync.dma_start(out=z_nat[:, k], in_=z_nat_v[:, k])
             if 0 <= k + 2 < NC:
@@ -320,6 +318,8 @@ def tile_rbf_kernel_v_kernel(tc, X, Z, l_raw, sigma_f_raw, arg, grad_out, out_0,
                 group_points(x_raw[:, k], "x%d" % k)
             if 0 <= k + 1 < NC:
                 mult(k + 1)
+            if 3 <= k + 4 < NC:
+                load(k + 4)
             if 0 <= k < NC:
                 keep_column_sums(k)
             if 0 <= k + 1 < NC:

from contextlib import ExitStack

import concourse.mybir as mybir
from concourse.masks import make_identity

N_TOK = 2048
N_FEAT = 2048
D = 512
FLOPS = 2 * 2 * N_TOK * N_FEAT * D

F32 = mybir.dt.float32
BF16 = mybir.dt.bfloat16
U32 = mybir.dt.uint32
U8 = mybir.dt.uint8
E4 = mybir.dt.float8_e4m3fn_x4
E5 = mybir.dt.float8_e5m2_x4
ALU = mybir.AluOpType
ACT = mybir.ActivationFunctionType
AX = mybir.AxisListType

P = 128
PACK = 4
GRP = 512
NG = 4
NC = NG * NG
LIM = 36.0
MX_PER_STEP = 3
LAST_SHARED_CAST = 13


def tile_rbf_kernel_v_kernel(tc, X, Z, l_raw, sigma_f_raw, arg, grad_out, out_0, out_1):
    nc = tc.nc

    x_v = X.rearrange("(g p t) d -> p g t d", p=P, t=PACK)
    z_v = Z.rearrange("(g p t) d -> p g t d", p=P, t=PACK)
    z_nat_v = Z.rearrange("(g b p) d -> p g b d", p=P, b=PACK)
    arg_v = arg.rearrange("(g p t) j -> p g t j", p=P, t=PACK)
    go_v = grad_out.rearrange("(g p t) j -> p g t j", p=P, t=PACK)
    o0_v = out_0.rearrange("(g p t) d -> p g t d", p=P, t=PACK)
    o1_v = out_1.rearrange("(g b p) d -> p g b d", p=P, b=PACK)

    order = []
    for s in range(NG):
        for G in range(s, NG):
            order.append((s, G))
        for g in range(s + 1, NG):
            order.append((g, s))
    row_done = {}
    col_done = {}
    row_count = [0] * NG
    col_count = [0] * NG
    for c, (g, G) in enumerate(order):
        row_count[g] = row_count[g] + 1
        col_count[G] = col_count[G] + 1
        if row_count[g] == NG:
            row_done[c] = g
        if col_count[G] == NG:
            col_done[c] = G

    with ExitStack() as ctx:
        const = ctx.enter_context(tc.tile_pool(name="const", bufs=1))
        keep = ctx.enter_context(tc.tile_pool(name="keep", bufs=1))
        stream = ctx.enter_context(tc.tile_pool(name="stream", bufs=2))
        ps_t = ctx.enter_context(tc.psum_pool(name="ps_t", bufs=4))
        ps_c = ctx.enter_context(tc.psum_pool(name="ps_c", bufs=1))
        ps_m = ctx.enter_context(tc.psum_pool(name="ps_m", bufs=3))
        ctx.enter_context(tc.manual_schedule())

        x_raw = keep.tile([P, NG, PACK, D], BF16, name="x_raw")
        z_nat = keep.tile([P, NG, PACK, D], BF16, name="z_nat")
        x_codes = keep.tile([P, NG, D], U32, name="x_codes", align_bytes=64)
        x_scales = keep.tile([P, NG, D], U8, name="x_scales", align_bytes=64)
        z_codes = keep.tile([P, NG, D], U32, name="z_codes", align_bytes=64)
        z_scales = keep.tile([P, NG, D], U8, name="z_scales", align_bytes=64)
        tok_codes = keep.tile([P, NG, N_FEAT], U32, name="tok_codes", align_bytes=64)
        tok_scales = keep.tile([P, NG, N_FEAT], U8, name="tok_scales", align_bytes=64)
        feat_codes = keep.tile([P, NG, N_TOK], U32, name="feat_codes", align_bytes=64)
        feat_scales = keep.tile([P, NG, N_TOK], U8, name="feat_scales", align_bytes=64)
        r_part = keep.tile([P, NG, PACK, NG], F32, name="r_part")
        c_part = keep.tile([P, NG, PACK, NG], F32, name="c_part")

        e_tiles = {}
        g_tiles = {}
        a_tiles = {}
        abf_tiles = {}
        grouped_tiles = {}
        fin_tiles = {}
        bank_tiles = {}
        c_banks = {}

        def load(c):
            g, G = order[c]
            cols = slice(G * GRP, (G + 1) * GRP)
            e_t = stream.tile([P, PACK, GRP], F32, name="e_t", tag="e_t", bufs=3)
            nc.sync.dma_start(out=e_t[:], in_=arg_v[:, g, :, cols])
            g_t = stream.tile([P, PACK, GRP], BF16, name="g_t", tag="g_t", bufs=3)
            nc.sync.dma_start(out=g_t[:], in_=go_v[:, g, :, cols])
            e_tiles[c] = e_t
            g_tiles[c] = g_t

        warm = const.tile([P, 1], F32, name="warm")
        nc.vector.memset(warm[:], 0.0)
        nc.scalar.activation(out=warm[:], in_=warm[:], func=ACT.Exp)
        lrow = const.tile([P, GRP + 32], BF16, name="lrow")
        nc.vector.memset(lrow[:], 0.0)
        nc.sync.dma_start(out=lrow[0:1, 0:GRP], in_=l_raw.rearrange("(o d) -> o d", o=1))
        nc.sync.dma_start(out=lrow[0:1, GRP:GRP + 1], in_=sigma_f_raw.rearrange("(o d) -> o d", o=1))
        ones_bf = const.tile([P, P], BF16, name="ones_bf")
        nc.vector.memset(ones_bf[:], 1.0)
        ident = const.tile([P, P], F32, name="ident")
        make_identity(nc, ident[:])

        z_tiles = {}

        def load_z(k):
            z_t = stream.tile([P, PACK, D], BF16, name="fin", tag="fin", bufs=2, align_bytes=64)
            nc.sync.dma_start(out=z_t[:], in_=z_v[:, k])
            z_tiles[k] = z_t

        def group_points(raw_k, key):
            grouped = stream.tile([P, D, PACK], BF16, name="grouped", tag="grouped", bufs=3, align_bytes=64)
            nc.vector.tensor_copy(
                out=grouped[:].rearrange("p (c i) t -> p c t i", i=4),
                in_=raw_k.rearrange("p t (c i) -> p c t i", i=4),
            )
            grouped_tiles[key] = grouped

        def quantize_points(key, codes, scales, k):
            nc.vector.quantize_mx(
                out=codes[:, k, :].bitcast(E4),
                scales=scales[:, k, :],
                in_=grouped_tiles[key][:].rearrange("p d t -> p (d t)"),
            )

        load_z(0)
        load_z(1)
        load(0)

        ps_l = ps_m.tile([P, D], F32, name="acc", tag="acc")
        nc.tensor.matmul(out=ps_l[:], lhsT=ones_bf[:], rhs=lrow[:, 0:GRP], start=True, stop=True)
        ps_s = ps_m.tile([P, D], F32, name="acc", tag="acc")
        nc.tensor.matmul(out=ps_s[:, 0:32], lhsT=ones_bf[:], rhs=lrow[:, GRP:GRP + 32], start=True, stop=True)
        v_sb = const.tile([P, GRP + 32], F32, name="v_sb")
        nc.vector.tensor_copy(out=v_sb[:, 0:GRP], in_=ps_l[:])
        nc.vector.tensor_copy(out=v_sb[:, GRP:GRP + 32], in_=ps_s[:, 0:32])
        sp = const.tile([P, GRP + 32], F32, name="sp")
        nc.vector.tensor_scalar_min(out=sp[:], in0=v_sb[:], scalar1=LIM)
        nc.scalar.activation(out=sp[:], in_=sp[:], func=ACT.Exp)
        nc.scalar.activation(out=sp[:], in_=sp[:], func=ACT.Ln, bias=1.0)

        group_points(z_tiles[0][:], "z0")
        group_points(z_tiles[1][:], "z1")
        load_z(2)
        load_z(3)
        load(1)
        nc.sync.dma_start(out=x_raw[:, 0], in_=x_v[:, 0])
        load(2)
        quantize_points("z0", z_codes, z_scales, 0)
        quantize_points("z1", z_codes, z_scales, 1)

        nc.vector.tensor_tensor(out=sp[:], in0=sp[:], in1=v_sb[:], op=ALU.max)
        sigma = const.tile([P, 1], F32, name="sigma")
        nc.vector.tensor_copy(out=sigma[:], in_=sp[:, GRP:GRP + 1])
        nc.vector.tensor_tensor(out=v_sb[:, 0:GRP], in0=sp[:, 0:GRP], in1=sp[:, 0:GRP], op=ALU.mult)
        w2n = const.tile([P, D], F32, name="w2n")
        nc.vector.reciprocal(out=w2n[:], in_=v_sb[:, 0:GRP])
        nc.vector.tensor_scalar_mul(out=w2n[:], in0=w2n[:], scalar1=-1.0)

        group_points(z_tiles[2][:], "z2")
        group_points(z_tiles[3][:], "z3")
        quantize_points("z2", z_codes, z_scales, 2)
        quantize_points("z3", z_codes, z_scales, 3)
        for k in range(1, NG):
            nc.sync.dma_start(out=x_raw[:, k], in_=x_v[:, k])

        def exp(c):
            nc.scalar.activation(out=e_tiles[c][:], in_=e_tiles[c][:], func=ACT.Exp)

        def mult(c):
            g, G = order[c]
            a32 = stream.tile([P, PACK, GRP], F32, name="a32", tag="a32", bufs=2)
            a_tiles[c] = a32
            for t in range(PACK):
                nc.vector.scalar_tensor_tensor(
                    out=a32[:, t, :], in0=e_tiles[c][:, t, :], scalar=sigma[:], in1=g_tiles[c][:, t, :],
                    op0=ALU.mult, op1=ALU.mult, accum_out=r_part[:, g, t, G:G + 1],
                )

        def cast_on_vector(c, h):
            return c < LAST_SHARED_CAST and (c % 2 == 0 or h == 1)

        def cast(c, on_vector):
            if c not in abf_tiles:
                abf = stream.tile([P, PACK, GRP], BF16, name="abf", tag="abf", bufs=2)
                abf_tiles[c] = abf
            for h in range(2):
                if cast_on_vector(c, h) == on_vector:
                    rows = slice(2 * h, 2 * h + 2)
                    if on_vector:
                        nc.vector.tensor_copy(out=abf_tiles[c][:, rows], in_=a_tiles[c][:, rows])
                    else:
                        nc.scalar.copy(out=abf_tiles[c][:, rows], in_=a_tiles[c][:, rows])

        def group_tokens(c):
            grouped = stream.tile([P, GRP, PACK], BF16, name="grouped", tag="grouped", bufs=3, align_bytes=64)
            grouped_tiles[c] = grouped
            nc.scalar.copy(
                out=grouped[:].rearrange("p (c i) t -> p c t i", i=4),
                in_=abf_tiles[c][:].rearrange("p t (c i) -> p c t i", i=4),
            )

        def quantize_tokens(c):
            g, G = order[c]
            cols = slice(G * GRP, (G + 1) * GRP)
            nc.vector.quantize_mx(
                out=tok_codes[:, g, cols].bitcast(E5),
                scales=tok_scales[:, g, cols],
                in_=grouped_tiles[c][:].rearrange("p c t -> p (c t)"),
            )

        def transposes(c):
            for h in range(2):
                bank = ps_t.tile([P, 2, 2, P], F32, name="bank", tag="bank")
                bank_tiles[(c, h)] = bank
                for t2 in range(2):
                    words = abf_tiles[c][:, 2 * h + t2, :].bitcast(F32)
                    for v in range(2):
                        nc.tensor.transpose(out=bank[:, t2, v, :], in_=words[:, v:GRP // 2:2], identity=ident[:])

        def column_sums(c):
            c_bank = ps_c.tile([P, PACK, P], F32, name="c_bank", tag="c_bank")
            c_banks[c] = c_bank
            for b in range(PACK):
                for t in range(PACK):
                    nc.tensor.matmul(
                        out=c_bank[:, b, :], lhsT=a_tiles[c][:, t, b * P:(b + 1) * P], rhs=ident[:],
                        is_transpose=True, start=(t == 0), stop=(t == PACK - 1),
                    )

        def keep_column_sums(c):
            g, G = order[c]
            nc.vector.tensor_reduce(out=c_part[:, G, :, g], in_=c_banks[c][:], axis=AX.X, op=ALU.add)

        def group_features(c):
            fin = stream.tile([P, PACK, P, PACK], BF16, name="fin", tag="fin", bufs=2, align_bytes=64)
            fin_tiles[c] = fin
            for h in range(2):
                fin_words = fin[:, 2 * h:2 * h + 2].rearrange("m t p u -> m (t p u)").bitcast(F32)
                nc.scalar.copy(
                    out=fin_words.rearrange("m (t p v) -> m t p v", t=2, v=2),
                    in_=bank_tiles[(c, h)][:].rearrange("m t v p -> m t p v"),
                )

        def quantize_features(c):
            g, G = order[c]
            rows = slice(g * GRP, (g + 1) * GRP)
            nc.vector.quantize_mx(
                out=feat_codes[:, G, rows].bitcast(E5),
                scales=feat_scales[:, G, rows],
                in_=fin_tiles[c][:].rearrange("m t p u -> m (t p u)"),
            )

        sums_tiles = {}

        def product(kind, s, t):
            if kind == 0:
                a_codes, a_scales, b_codes, b_scales, part = feat_codes, feat_scales, z_codes, z_scales, r_part
            else:
                a_codes, a_scales, b_codes, b_scales, part = tok_codes, tok_scales, x_codes, x_scales, c_part
            if t == 0:
                sums = stream.tile([P, PACK], F32, name="sums", tag="sums", bufs=3)
                nc.vector.tensor_reduce(out=sums[:], in_=part[:, s], axis=AX.X, op=ALU.add)
                sums_tiles[(kind, s)] = sums
            m_cols = slice(s * GRP + t * P, s * GRP + (t + 1) * P)
            acc = ps_m.tile([P, D], F32, name="acc", tag="acc")
            for k in range(NG):
                nc.tensor.matmul_mx(
                    out=acc[:],
                    lhsT=a_codes[:, k, m_cols].bitcast(E5), lhsT_scale=a_scales[:, k, m_cols],
                    rhs=b_codes[:, k, :].bitcast(E4), rhs_scale=b_scales[:, k, :],
                    start=(k == 0), stop=(k == NG - 1),
                )
            return (kind, s, t, acc)

        def subtract_sum_term(item):
            kind, s, t, acc = item
            raw = x_raw if kind == 0 else z_nat
            diff = stream.tile([P, D], F32, name="diff", tag="diff", bufs=3)
            nc.vector.scalar_tensor_tensor(
                out=diff[:], in0=raw[:, s, t, :], scalar=sums_tiles[(kind, s)][:, t:t + 1], in1=acc[:],
                op0=ALU.mult, op1=ALU.subtract,
            )
            return (kind, s, t, diff)

        def scale_and_store(item):
            kind, s, t, diff = item
            out_v = o0_v if kind == 0 else o1_v
            res = stream.tile([P, D], F32, name="res", tag="res", bufs=4)
            nc.vector.tensor_tensor(out=res[:], in0=diff[:], in1=w2n[:], op=ALU.mult)
            nc.sync.dma_start(out=out_v[:, s, t, :], in_=res[:])

        ready = []
        in_flight = []
        k = -2
        while k < NC + 1 or ready or in_flight:
            if 0 <= k < NG:
                nc.sync.dma_start(out=z_nat[:, k], in_=z_nat_v[:, k])
            if 0 <= k + 2 < NC:
                exp(k + 2)
            if 0 <= k < NC:
                transposes(k)
            if 0 <= k - 1 < NC:
                quantize_features(k - 1)
                if (k - 1) in row_done:
                    for t in range(PACK):
                        ready.append((0, row_done[k - 1], t))
            if 0 <= k < NG:
                group_points(x_raw[:, k], "x%d" % k)
            if 0 <= k + 1 < NC:
                mult(k + 1)
            if 3 <= k + 4 < NC:
                load(k + 4)
            if 0 <= k < NC:
                keep_column_sums(k)
            if 0 <= k + 1 < NC:
                column_sums(k + 1)
            if 0 <= k < NC:
                group_tokens(k)
            if 0 <= k < NG:
                quantize_points("x%d" % k, x_codes, x_scales, k)
            waiting = []
            for item in in_flight:
                waiting.append(subtract_sum_term(item))
                if len(waiting) > 1:
                    scale_and_store(waiting.pop(0))
            in_flight = []
            if 0 <= k + 1 < NC:
                cast(k + 1, True)
            if waiting:
                scale_and_store(waiting.pop(0))
            if 0 <= k < NC:
                quantize_tokens(k)
                if k in col_done:
                    for t in range(PACK):
                        ready.append((1, col_done[k], t))
            while ready and len(in_flight) < (2 if k < 12 else MX_PER_STEP):
                kind, s, t = ready.pop(0)
                in_flight.append(product(kind, s, t))
            if 0 <= k < NC:
                group_features(k)
            if 0 <= k + 1 < NC:
                cast(k + 1, False)
            k = k + 1
